import numpy as np
import ml_dtypes

BF16 = ml_dtypes.bfloat16


def bf(x):
    return np.asarray(x, np.float32).astype(BF16)


def f32(x):
    return np.asarray(x, np.float32)


def f64(x):
    return np.asarray(x).astype(np.float64)


def striped(idx):
    return np.tile(idx.reshape(-1, 16).T, (8, 1))


S, D, M, N = 512, 128, 256, 256


def elu(v):
    return np.maximum(v, 0.0) + np.exp(np.minimum(v, 0.0)) - 1.0


def setup_inputs():
    return {"table": bf(np.random.standard_normal((S, D))), "w_t": bf(np.random.standard_normal((D, M)) / np.sqrt(D + D + D)), "u": bf(np.random.standard_normal((D, N))), "w_u": bf(np.random.standard_normal((D, M)) / np.sqrt(D + D + D)), "ctx": f32(0.6 * np.random.standard_normal((M, 1))), "offs": striped(np.random.permutation(np.tile(np.arange(S), 2))[:N])}


def reference(table, w_t, u, w_u, ctx, offs):
    idx = offs[:16].T.reshape(-1)
    v = f64(w_t).T @ f64(table)[idx].T + f64(w_u).T @ f64(u) + f64(ctx)
    return elu(v)

@@ -1,0 +1,76 @@
+import concourse.mybir as mybir
+from concourse.masks import make_identity
+
+P = 128
+S, D, M, N = 512, 128, 256, 256
+FLOPS = 2 * (D + D) * M * N
+
+BF16, F32, U16 = mybir.dt.bfloat16, mybir.dt.float32, mybir.dt.uint16
+ADD, MAX, MIN = mybir.AluOpType.add, mybir.AluOpType.max, mybir.AluOpType.min
+EXP = mybir.ActivationFunctionType.Exp
+
+
+def tile_actorcritic_kernel(tc, table, w_t, u, w_u, ctx, offs, out):
+    nc = tc.nc
+    task_blocks = S // P
+    out_blocks = M // P
+
+    with (
+        tc.tile_pool(name="held", bufs=1) as held,
+        tc.psum_pool(name="psum", bufs=1) as psum,
+    ):
+        offsets = held.tile([P, N // 16], U16, name="offsets")
+        nc.sync.dma_start(offsets[:], offs)
+
+        rows = []
+        for a in range(task_blocks):
+            block = held.tile([P, D], BF16, name=f"rows{a}")
+            nc.sync.dma_start(block[:], table[a * P : (a + 1) * P, :])
+            rows.append(block)
+
+        u_sb = held.tile([D, N], BF16, name="u_sb")
+        nc.scalar.dma_start(u_sb[:], u)
+        w_u_sb = held.tile([D, M], BF16, name="w_u_sb")
+        nc.scalar.dma_start(w_u_sb[:], w_u)
+        w_t_sb = held.tile([D, M], BF16, name="w_t_sb")
+        nc.scalar.dma_start(w_t_sb[:], w_t)
+
+        shift = []
+        for b in range(out_blocks):
+            column = held.tile([P, 1], F32, name=f"shift{b}")
+            nc.gpsimd.dma_start(column[:], ctx[b * P : (b + 1) * P, :])
+            shift.append(column)
+
+        identity = held.tile([P, P], BF16, name="identity")
+        make_identity(nc, identity[:])
+
+        acc = []
+        for b in range(out_blocks):
+            bank = psum.tile([P, N], F32, name=f"acc{b}")
+            nc.tensor.matmul(bank[:], w_u_sb[:, b * P : (b + 1) * P], u_sb[:], start=True, stop=False)
+            acc.append(bank)
+
+        turned = psum.tile([D, S], BF16, name="turned")
+        for a in range(task_blocks):
+            nc.tensor.transpose(turned[:, a * P : (a + 1) * P], rows[a][:], identity[:])
+        window = held.tile([D, S], BF16, name="window")
+        nc.vector.tensor_copy(window[:], turned[:])
+
+        for b in range(out_blocks):
+            nc.tensor.matmul(
+                acc[b][:],
+                w_t_sb[:, b * P : (b + 1) * P],
+                window[:].indirect(offsets[:]),
+                start=False,
+                stop=True,
+            )
+
+        for b in range(out_blocks):
+            below = held.tile([P, N], F32, name=f"below{b}")
+            nc.vector.tensor_scalar(below[:], acc[b][:], shift[b][:], 0.0, ADD, MIN)
+            nc.scalar.activation(below[:], below[:], EXP)
+            above = held.tile([P, N], F32, name=f"above{b}")
+            nc.vector.tensor_scalar(above[:], acc[b][:], shift[b][:], 0.0, ADD, MAX)
+            result = held.tile([P, N], F32, name=f"result{b}")
+            nc.vector.scalar_tensor_tensor(result[:], below[:], -1.0, above[:], ADD, ADD)
+            nc.sync.dma_start(out[b * P : (b + 1) * P, :], result[:])

@@ -12,24 +12,29 @@ EXP = mybir.ActivationFunctionType.Exp
 
 def tile_actorcritic_kernel(tc, table, w_t, u, w_u, ctx, offs, out):
     nc = tc.nc
-    task_blocks = S // P
+    halves = 2
+    blocks_per_half = S // P // halves
     out_blocks = M // P
 
     with (
         tc.tile_pool(name="held", bufs=1) as held,
         tc.psum_pool(name="psum", bufs=1) as psum,
     ):
+        identity = held.tile([P, P], BF16, name="identity")
+        make_identity(nc, identity[:])
+
+        rows = []
+        for h, queue in enumerate((nc.sync, nc.scalar)):
+            half = held.tile([P, blocks_per_half, D], BF16, name=f"rows{h}")
+            tasks = table[h * blocks_per_half * P : (h + 1) * blocks_per_half * P, :]
+            queue.dma_start(half[:], tasks.rearrange("(a p) d -> p a d", p=P))
+            rows.append(half)
+
         offsets = held.tile([P, N // 16], U16, name="offsets")
         nc.sync.dma_start(offsets[:], offs)
 
-        rows = []
-        for a in range(task_blocks):
-            block = held.tile([P, D], BF16, name=f"rows{a}")
-            nc.sync.dma_start(block[:], table[a * P : (a + 1) * P, :])
-            rows.append(block)
-
         u_sb = held.tile([D, N], BF16, name="u_sb")
-        nc.scalar.dma_start(u_sb[:], u)
+        nc.sync.dma_start(u_sb[:], u)
         w_u_sb = held.tile([D, M], BF16, name="w_u_sb")
         nc.scalar.dma_start(w_u_sb[:], w_u)
         w_t_sb = held.tile([D, M], BF16, name="w_t_sb")
@@ -38,23 +43,22 @@ def tile_actorcritic_kernel(tc, table, w_t, u, w_u, ctx, offs, out):
         shift = []
         for b in range(out_blocks):
             column = held.tile([P, 1], F32, name=f"shift{b}")
-            nc.gpsimd.dma_start(column[:], ctx[b * P : (b + 1) * P, :])
+            nc.sync.dma_start(column[:], ctx[b * P : (b + 1) * P, :])
             shift.append(column)
 
-        identity = held.tile([P, P], BF16, name="identity")
-        make_identity(nc, identity[:])
+        turned = psum.tile([D, S], BF16, name="turned")
+        for h in range(halves):
+            for a in range(blocks_per_half):
+                first = (h * blocks_per_half + a) * P
+                nc.tensor.transpose(turned[:, first : first + P], rows[h][:, a, :], identity[:])
+        window = held.tile([D, S], BF16, name="window")
+        nc.vector.tensor_copy(window[:], turned[:])
 
         acc = []
         for b in range(out_blocks):
             bank = psum.tile([P, N], F32, name=f"acc{b}")
             nc.tensor.matmul(bank[:], w_u_sb[:, b * P : (b + 1) * P], u_sb[:], start=True, stop=False)
             acc.append(bank)
-
-        turned = psum.tile([D, S], BF16, name="turned")
-        for a in range(task_blocks):
-            nc.tensor.transpose(turned[:, a * P : (a + 1) * P], rows[a][:], identity[:])
-        window = held.tile([D, S], BF16, name="window")
-        nc.vector.tensor_copy(window[:], turned[:])
 
         for b in range(out_blocks):
             nc.tensor.matmul(

@@ -13,7 +13,7 @@ EXP = mybir.ActivationFunctionType.Exp
 def tile_actorcritic_kernel(tc, table, w_t, u, w_u, ctx, offs, out):
     nc = tc.nc
     halves = 2
-    blocks_per_half = S // P // halves
+    pair = S // halves // P
     out_blocks = M // P
 
     with (
@@ -25,9 +25,9 @@ def tile_actorcritic_kernel(tc, table, w_t, u, w_u, ctx, offs, out):
 
         rows = []
         for h, queue in enumerate((nc.sync, nc.scalar)):
-            half = held.tile([P, blocks_per_half, D], BF16, name=f"rows{h}")
-            tasks = table[h * blocks_per_half * P : (h + 1) * blocks_per_half * P, :]
-            queue.dma_start(half[:], tasks.rearrange("(a p) d -> p a d", p=P))
+            half = held.tile([P, pair, D], BF16, name=f"rows{h}")
+            tasks = table[h * pair * P : (h + 1) * pair * P, :]
+            queue.dma_start(half[:], tasks.rearrange("(p a) d -> p a d", a=pair))
             rows.append(half)
 
         offsets = held.tile([P, N // 16], U16, name="offsets")
@@ -35,10 +35,10 @@ def tile_actorcritic_kernel(tc, table, w_t, u, w_u, ctx, offs, out):
 
         u_sb = held.tile([D, N], BF16, name="u_sb")
         nc.sync.dma_start(u_sb[:], u)
-        w_u_sb = held.tile([D, M], BF16, name="w_u_sb")
-        nc.scalar.dma_start(w_u_sb[:], w_u)
         w_t_sb = held.tile([D, M], BF16, name="w_t_sb")
         nc.scalar.dma_start(w_t_sb[:], w_t)
+        w_u_sb = held.tile([D, M], BF16, name="w_u_sb")
+        nc.scalar.dma_start(w_u_sb[:], w_u)
 
         shift = []
         for b in range(out_blocks):
@@ -46,35 +46,35 @@ def tile_actorcritic_kernel(tc, table, w_t, u, w_u, ctx, offs, out):
             nc.sync.dma_start(column[:], ctx[b * P : (b + 1) * P, :])
             shift.append(column)
 
-        turned = psum.tile([D, S], BF16, name="turned")
-        for h in range(halves):
-            for a in range(blocks_per_half):
-                first = (h * blocks_per_half + a) * P
-                nc.tensor.transpose(turned[:, first : first + P], rows[h][:, a, :], identity[:])
         window = held.tile([D, S], BF16, name="window")
-        nc.vector.tensor_copy(window[:], turned[:])
+        for h, copy in enumerate((nc.scalar.copy, nc.vector.tensor_copy)):
+            turned = psum.tile([D, pair * P], BF16, name=f"turned{h}")
+            for a in range(pair):
+                nc.tensor.transpose(turned[:, a * P : (a + 1) * P], rows[h][:, a, :], identity[:])
+            copy(
+                window[:, h * pair * P : (h + 1) * pair * P].rearrange("d (p a) -> d p a", a=pair),
+                turned[:].rearrange("d (a p) -> d p a", a=pair),
+            )
 
         acc = []
         for b in range(out_blocks):
             bank = psum.tile([P, N], F32, name=f"acc{b}")
-            nc.tensor.matmul(bank[:], w_u_sb[:, b * P : (b + 1) * P], u_sb[:], start=True, stop=False)
-            acc.append(bank)
-
-        for b in range(out_blocks):
             nc.tensor.matmul(
-                acc[b][:],
+                bank[:],
                 w_t_sb[:, b * P : (b + 1) * P],
                 window[:].indirect(offsets[:]),
-                start=False,
-                stop=True,
+                start=True,
+                stop=False,
             )
+            acc.append(bank)
+        for b in range(out_blocks):
+            nc.tensor.matmul(acc[b][:], w_u_sb[:, b * P : (b + 1) * P], u_sb[:], start=False, stop=True)
 
         for b in range(out_blocks):
-            below = held.tile([P, N], F32, name=f"below{b}")
-            nc.vector.tensor_scalar(below[:], acc[b][:], shift[b][:], 0.0, ADD, MIN)
-            nc.scalar.activation(below[:], below[:], EXP)
-            above = held.tile([P, N], F32, name=f"above{b}")
-            nc.vector.tensor_scalar(above[:], acc[b][:], shift[b][:], 0.0, ADD, MAX)
+            grown = held.tile([P, N], F32, name=f"grown{b}")
+            nc.scalar.activation(grown[:], acc[b][:], EXP, bias=shift[b][:])
+            curve = held.tile([P, N], F32, name=f"curve{b}")
+            nc.vector.tensor_scalar(curve[:], grown[:], 1.0, -1.0, MIN, ADD)
             result = held.tile([P, N], F32, name=f"result{b}")
-            nc.vector.scalar_tensor_tensor(result[:], below[:], -1.0, above[:], ADD, ADD)
+            nc.vector.scalar_tensor_tensor(result[:], acc[b][:], shift[b][:], curve[:], ADD, MAX)
             nc.sync.dma_start(out[b * P : (b + 1) * P, :], result[:])

@@ -4,6 +4,7 @@ from concourse.masks import make_identity
 P = 128
 S, D, M, N = 512, 128, 256, 256
 FLOPS = 2 * (D + D) * M * N
+WARM_MATMULS = 12
 
 BF16, F32, U16 = mybir.dt.bfloat16, mybir.dt.float32, mybir.dt.uint16
 ADD, MAX, MIN = mybir.AluOpType.add, mybir.AluOpType.max, mybir.AluOpType.min
@@ -20,6 +21,12 @@ def tile_actorcritic_kernel(tc, table, w_t, u, w_u, ctx, offs, out):
         tc.tile_pool(name="held", bufs=1) as held,
         tc.psum_pool(name="psum", bufs=1) as psum,
     ):
+        zeros = held.tile([P, P], BF16, name="zeros")
+        nc.vector.memset(zeros[:], 0.0)
+        unread = psum.tile([P, P], F32, name="unread")
+        for k in range(WARM_MATMULS):
+            nc.tensor.matmul(unread[:], zeros[:], zeros[:], start=True, stop=True)
+
         identity = held.tile([P, P], BF16, name="identity")
         make_identity(nc, identity[:])
 

@@ -4,7 +4,6 @@ from concourse.masks import make_identity
 P = 128
 S, D, M, N = 512, 128, 256, 256
 FLOPS = 2 * (D + D) * M * N
-WARM_MATMULS = 12
 
 BF16, F32, U16 = mybir.dt.bfloat16, mybir.dt.float32, mybir.dt.uint16
 ADD, MAX, MIN = mybir.AluOpType.add, mybir.AluOpType.max, mybir.AluOpType.min
@@ -21,12 +20,6 @@ def tile_actorcritic_kernel(tc, table, w_t, u, w_u, ctx, offs, out):
         tc.tile_pool(name="held", bufs=1) as held,
         tc.psum_pool(name="psum", bufs=1) as psum,
     ):
-        zeros = held.tile([P, P], BF16, name="zeros")
-        nc.vector.memset(zeros[:], 0.0)
-        unread = psum.tile([P, P], F32, name="unread")
-        for k in range(WARM_MATMULS):
-            nc.tensor.matmul(unread[:], zeros[:], zeros[:], start=True, stop=True)
-
         identity = held.tile([P, P], BF16, name="identity")
         make_identity(nc, identity[:])
 
@@ -34,7 +27,7 @@ def tile_actorcritic_kernel(tc, table, w_t, u, w_u, ctx, offs, out):
         for h, queue in enumerate((nc.sync, nc.scalar)):
             half = held.tile([P, pair, D], BF16, name=f"rows{h}")
             tasks = table[h * pair * P : (h + 1) * pair * P, :]
-            queue.dma_start(half[:], tasks.rearrange("(p a) d -> p a d", a=pair))
+            queue.dma_start(half[:], tasks.rearrange("(a p) d -> p a d", a=pair))
             rows.append(half)
 
         offsets = held.tile([P, N // 16], U16, name="offsets")
@@ -58,10 +51,7 @@ def tile_actorcritic_kernel(tc, table, w_t, u, w_u, ctx, offs, out):
             turned = psum.tile([D, pair * P], BF16, name=f"turned{h}")
             for a in range(pair):
                 nc.tensor.transpose(turned[:, a * P : (a + 1) * P], rows[h][:, a, :], identity[:])
-            copy(
-                window[:, h * pair * P : (h + 1) * pair * P].rearrange("d (p a) -> d p a", a=pair),
-                turned[:].rearrange("d (a p) -> d p a", a=pair),
-            )
+            copy(window[:, h * pair * P : (h + 1) * pair * P], turned[:])
 
         acc = []
         for b in range(out_blocks):

@@ -48,24 +48,24 @@ def tile_actorcritic_kernel(tc, table, w_t, u, w_u, ctx, offs, out):
 
         window = held.tile([D, S], BF16, name="window")
         for h, copy in enumerate((nc.scalar.copy, nc.vector.tensor_copy)):
-            turned = psum.tile([D, pair * P], BF16, name=f"turned{h}")
+            turned = psum.tile([D, pair * P], BF16, name=f"turned{h}", tag=f"bank{h}")
             for a in range(pair):
                 nc.tensor.transpose(turned[:, a * P : (a + 1) * P], rows[h][:, a, :], identity[:])
             copy(window[:, h * pair * P : (h + 1) * pair * P], turned[:])
 
         acc = []
         for b in range(out_blocks):
-            bank = psum.tile([P, N], F32, name=f"acc{b}")
-            nc.tensor.matmul(
-                bank[:],
-                w_t_sb[:, b * P : (b + 1) * P],
-                window[:].indirect(offsets[:]),
-                start=True,
-                stop=False,
-            )
+            bank = psum.tile([P, N], F32, name=f"acc{b}", tag=f"bank{b}")
+            nc.tensor.matmul(bank[:], w_u_sb[:, b * P : (b + 1) * P], u_sb[:], start=True, stop=False)
             acc.append(bank)
         for b in range(out_blocks):
-            nc.tensor.matmul(acc[b][:], w_u_sb[:, b * P : (b + 1) * P], u_sb[:], start=False, stop=True)
+            nc.tensor.matmul(
+                acc[b][:],
+                w_t_sb[:, b * P : (b + 1) * P],
+                window[:].indirect(offsets[:]),
+                start=False,
+                stop=True,
+            )
 
         for b in range(out_blocks):
             grown = held.tile([P, N], F32, name=f"grown{b}")

@@ -47,11 +47,11 @@ def tile_actorcritic_kernel(tc, table, w_t, u, w_u, ctx, offs, out):
             shift.append(column)
 
         window = held.tile([D, S], BF16, name="window")
-        for h, copy in enumerate((nc.scalar.copy, nc.vector.tensor_copy)):
-            turned = psum.tile([D, pair * P], BF16, name=f"turned{h}", tag=f"bank{h}")
-            for a in range(pair):
-                nc.tensor.transpose(turned[:, a * P : (a + 1) * P], rows[h][:, a, :], identity[:])
-            copy(window[:, h * pair * P : (h + 1) * pair * P], turned[:])
+        for k in range(S // P):
+            turned = psum.tile([D, P], BF16, name=f"turned{k}", tag=f"bank{k}")
+            nc.tensor.transpose(turned[:], rows[k // pair][:, k % pair, :], identity[:])
+            copy = nc.scalar.copy if k % 2 == 0 else nc.vector.tensor_copy
+            copy(window[:, k * P : (k + 1) * P], turned[:])
 
         acc = []
         for b in range(out_blocks):

@@ -46,12 +46,15 @@ def tile_actorcritic_kernel(tc, table, w_t, u, w_u, ctx, offs, out):
             nc.sync.dma_start(column[:], ctx[b * P : (b + 1) * P, :])
             shift.append(column)
 
+        spark = held.tile([P, 1], F32, name="spark")
+        nc.vector.memset(spark[:], 0.0)
+        nc.scalar.activation(spark[:], spark[:], EXP)
+
         window = held.tile([D, S], BF16, name="window")
         for k in range(S // P):
             turned = psum.tile([D, P], BF16, name=f"turned{k}", tag=f"bank{k}")
             nc.tensor.transpose(turned[:], rows[k // pair][:, k % pair, :], identity[:])
-            copy = nc.scalar.copy if k % 2 == 0 else nc.vector.tensor_copy
-            copy(window[:, k * P : (k + 1) * P], turned[:])
+            nc.vector.tensor_copy(window[:, k * P : (k + 1) * P], turned[:])
 
         acc = []
         for b in range(out_blocks):

@@ -12,8 +12,6 @@ EXP = mybir.ActivationFunctionType.Exp
 
 def tile_actorcritic_kernel(tc, table, w_t, u, w_u, ctx, offs, out):
     nc = tc.nc
-    halves = 2
-    pair = S // halves // P
     out_blocks = M // P
 
     with (
@@ -24,11 +22,10 @@ def tile_actorcritic_kernel(tc, table, w_t, u, w_u, ctx, offs, out):
         make_identity(nc, identity[:])
 
         rows = []
-        for h, queue in enumerate((nc.sync, nc.scalar)):
-            half = held.tile([P, pair, D], BF16, name=f"rows{h}")
-            tasks = table[h * pair * P : (h + 1) * pair * P, :]
-            queue.dma_start(half[:], tasks.rearrange("(a p) d -> p a d", a=pair))
-            rows.append(half)
+        for k in range(S // P):
+            block = held.tile([P, D], BF16, name=f"rows{k}")
+            (nc.sync, nc.scalar)[k % 2].dma_start(block[:], table[k * P : (k + 1) * P, :])
+            rows.append(block)
 
         offsets = held.tile([P, N // 16], U16, name="offsets")
         nc.sync.dma_start(offsets[:], offs)
@@ -53,7 +50,7 @@ def tile_actorcritic_kernel(tc, table, w_t, u, w_u, ctx, offs, out):
         window = held.tile([D, S], BF16, name="window")
         for k in range(S // P):
             turned = psum.tile([D, P], BF16, name=f"turned{k}", tag=f"bank{k}")
-            nc.tensor.transpose(turned[:], rows[k // pair][:, k % pair, :], identity[:])
+            nc.tensor.transpose(turned[:], rows[k][:], identity[:])
             nc.vector.tensor_copy(window[:, k * P : (k + 1) * P], turned[:])
 
         acc = []

@@ -27,15 +27,15 @@ def tile_actorcritic_kernel(tc, table, w_t, u, w_u, ctx, offs, out):
             (nc.sync, nc.scalar)[k % 2].dma_start(block[:], table[k * P : (k + 1) * P, :])
             rows.append(block)
 
-        offsets = held.tile([P, N // 16], U16, name="offsets")
-        nc.sync.dma_start(offsets[:], offs)
-
         u_sb = held.tile([D, N], BF16, name="u_sb")
         nc.sync.dma_start(u_sb[:], u)
-        w_t_sb = held.tile([D, M], BF16, name="w_t_sb")
-        nc.scalar.dma_start(w_t_sb[:], w_t)
         w_u_sb = held.tile([D, M], BF16, name="w_u_sb")
         nc.scalar.dma_start(w_u_sb[:], w_u)
+
+        offsets = held.tile([P, N // 16], U16, name="offsets")
+        nc.sync.dma_start(offsets[:], offs)
+        w_t_sb = held.tile([D, M], BF16, name="w_t_sb")
+        nc.scalar.dma_start(w_t_sb[:], w_t)
 
         shift = []
         for b in range(out_blocks):

import concourse.mybir as mybir
from concourse.masks import make_identity

P = 128
S, D, M, N = 512, 128, 256, 256
FLOPS = 2 * (D + D) * M * N

BF16, F32, U16 = mybir.dt.bfloat16, mybir.dt.float32, mybir.dt.uint16
ADD, MAX, MIN = mybir.AluOpType.add, mybir.AluOpType.max, mybir.AluOpType.min
EXP = mybir.ActivationFunctionType.Exp


def tile_actorcritic_kernel(tc, table, w_t, u, w_u, ctx, offs, out):
    nc = tc.nc
    out_blocks = M // P

    with (
        tc.tile_pool(name="held", bufs=1) as held,
        tc.psum_pool(name="psum", bufs=1) as psum,
    ):
        identity = held.tile([P, P], BF16, name="identity")
        make_identity(nc, identity[:])

        rows = []
        for k in range(S // P):
            block = held.tile([P, D], BF16, name=f"rows{k}")
            (nc.sync, nc.scalar)[k % 2].dma_start(block[:], table[k * P : (k + 1) * P, :])
            rows.append(block)

        u_sb = held.tile([D, N], BF16, name="u_sb")
        nc.sync.dma_start(u_sb[:], u)
        w_u_sb = held.tile([D, M], BF16, name="w_u_sb")
        nc.scalar.dma_start(w_u_sb[:], w_u)

        offsets = held.tile([P, N // 16], U16, name="offsets")
        nc.sync.dma_start(offsets[:], offs)
        w_t_sb = held.tile([D, M], BF16, name="w_t_sb")
        nc.scalar.dma_start(w_t_sb[:], w_t)

        shift = []
        for b in range(out_blocks):
            column = held.tile([P, 1], F32, name=f"shift{b}")
            nc.sync.dma_start(column[:], ctx[b * P : (b + 1) * P, :])
            shift.append(column)

        spark = held.tile([P, 1], F32, name="spark")
        nc.vector.memset(spark[:], 0.0)
        nc.scalar.activation(spark[:], spark[:], EXP)

        window = held.tile([D, S], BF16, name="window")
        for k in range(S // P):
            turned = psum.tile([D, P], BF16, name=f"turned{k}", tag=f"bank{k}")
            nc.tensor.transpose(turned[:], rows[k][:], identity[:])
            nc.vector.tensor_copy(window[:, k * P : (k + 1) * P], turned[:])

        acc = []
        for b in range(out_blocks):
            bank = psum.tile([P, N], F32, name=f"acc{b}", tag=f"bank{b}")
            nc.tensor.matmul(bank[:], w_u_sb[:, b * P : (b + 1) * P], u_sb[:], start=True, stop=False)
            acc.append(bank)
        for b in range(out_blocks):
            nc.tensor.matmul(
                acc[b][:],
                w_t_sb[:, b * P : (b + 1) * P],
                window[:].indirect(offsets[:]),
                start=False,
                stop=True,
            )

        for b in range(out_blocks):
            grown = held.tile([P, N], F32, name=f"grown{b}")
            nc.scalar.activation(grown[:], acc[b][:], EXP, bias=shift[b][:])
            curve = held.tile([P, N], F32, name=f"curve{b}")
            nc.vector.tensor_scalar(curve[:], grown[:], 1.0, -1.0, MIN, ADD)
            result = held.tile([P, N], F32, name=f"result{b}")
            nc.vector.scalar_tensor_tensor(result[:], acc[b][:], shift[b][:], curve[:], ADD, MAX)
            nc.sync.dma_start(out[b * P : (b + 1) * P, :], result[:])
